import numpy as np
import ml_dtypes


def mxq(x, axis, fmt="e4m3"):
    dtype, down = {"e4m3": (ml_dtypes.float8_e4m3fn, 7), "e5m2": (ml_dtypes.float8_e5m2, 14)}[fmt]
    v = np.moveaxis(np.asarray(x, np.float32).astype(ml_dtypes.bfloat16).astype(np.float64), axis, -1)
    blocks = v.reshape(v.shape[:-1] + (-1, 32))
    amax = np.abs(blocks).max(-1, keepdims=True)
    byte = np.maximum(np.where(amax > 0, np.frexp(amax)[1] - 1 + 127, 0) - down, 1)
    scale = np.exp2(byte - 127.0)
    codes = (blocks / scale).astype(np.float32).astype(dtype).astype(np.float64)
    return np.moveaxis((codes * scale).reshape(v.shape), -1, axis)


WIDE = False


def mx_kscale(k):
    if not WIDE:
        return np.ones(k)
    levels = np.array([10, -10, 5, -5, 0])
    a = np.random.permutation(np.resize(levels, k // 512 * 4)).reshape(k // 512, 4)
    idx = np.arange(k)
    return np.exp2(a[idx // 512, idx % 128 // 32])


BF16 = ml_dtypes.bfloat16


def bf(x):
    return np.asarray(x, np.float32).astype(BF16)


def f64(x):
    return np.asarray(x).astype(np.float64)


N, D, M, P = 4096, 8, 1024, 1024


def setup_inputs():
    a = np.log2(mx_kscale(M))
    a = a.max() - a
    x = np.random.standard_normal((N, D))
    z = np.random.uniform(0.0, 1.0, (M, D))
    z[:, 0] += a * np.log(2.0)
    g = np.random.standard_normal((M, P)) * 3.2 / np.sqrt(M)
    c = np.triu(g) + 0.25 * np.tril(g, -1) + np.eye(M, P)
    return {"x": bf(x), "design_points": bf(z), "chol_inv": bf(c * np.exp2(a)[:, None])}


def reference(x, design_points, chol_inv):
    x = f64(x)
    z = f64(design_points)
    mn = np.min(x, axis=0, keepdims=True)
    mx = np.max(x, axis=0, keepdims=True)
    xs = (x - mn) / (mx - mn)
    l1 = np.zeros((x.shape[0], z.shape[0]))
    for d in range(D):
        l1 = l1 + np.abs(xs[:, d][:, None] - z[:, d][None, :])
    k_star = np.exp(-l1)
    return mxq(k_star, 1, "e4m3") @ mxq(f64(chol_inv), 0, "e4m3")

@@ -1,0 +1,280 @@
+from contextlib import ExitStack
+
+import concourse.mybir as mybir
+from concourse.masks import make_identity
+
+F32 = mybir.dt.float32
+BF16 = mybir.dt.bfloat16
+U32 = mybir.dt.uint32
+U8 = mybir.dt.uint8
+FP8X4 = mybir.dt.float8_e4m3fn_x4
+ALU = mybir.AluOpType
+ACTF = mybir.ActivationFunctionType
+AX = mybir.AxisListType
+
+P = 128
+N_ROWS = 4096
+D = 8
+M = 1024
+COLS = 1024
+NT = N_ROWS // P
+PACK = 4
+PASSES = M // (P * PACK)
+HALF = 512
+FLOPS = 2 * N_ROWS * M * COLS
+
+
+def config(j):
+    return (3, 3, 2)
+
+
+def tile_tmgp_sg_kernel(tc, x, design_points, chol_inv, out):
+    nc = tc.nc
+    with ExitStack() as ctx:
+        const = ctx.enter_context(tc.tile_pool(name="const", bufs=1))
+        terms_pool = ctx.enter_context(tc.tile_pool(name="terms", bufs=3))
+        work = ctx.enter_context(tc.tile_pool(name="work", bufs=3))
+        ps_l = ctx.enter_context(tc.psum_pool(name="ps_l", bufs=4))
+        ps_o = ctx.enter_context(tc.psum_pool(name="ps_o", bufs=4))
+
+        xb = const.tile([P, NT, D], BF16, name="xb")
+        nc.sync.dma_start(out=xb[:], in_=x.rearrange("(p j) d -> p j d", j=NT))
+        zb = const.tile([P, PASSES, PACK, D], BF16, name="zb")
+        nc.sync.dma_start(
+            out=zb[:],
+            in_=design_points.rearrange("(g p t) d -> p g t d", g=PASSES, t=PACK),
+        )
+        craw = const.tile([P, PASSES, PACK, COLS], BF16, name="craw")
+        c_view = chol_inv.rearrange("(g p t) c -> g p t c", g=PASSES, t=PACK)
+        for g in range(PASSES):
+            nc.sync.dma_start(out=craw[:, g], in_=c_view[g])
+
+        ident = const.tile([P, P], F32, name="ident")
+        make_identity(nc, ident[:])
+
+        stat = const.tile([P, P], F32, name="stat")
+        nc.vector.memset(stat[:], 0.0)
+        x_by_d = xb[:].rearrange("p j d -> p d j")
+        nc.vector.tensor_reduce(out=stat[:, 0:D], in_=x_by_d, axis=AX.X, op=ALU.max)
+        mn_part = const.tile([P, D], F32, name="mn_part")
+        nc.vector.tensor_reduce(out=mn_part[:], in_=x_by_d, axis=AX.X, op=ALU.min)
+        nc.vector.tensor_scalar(
+            out=stat[:, D : 2 * D], in0=mn_part[:], scalar1=-1.0, scalar2=None, op0=ALU.mult
+        )
+        stat_t = ps_l.tile([P, P], F32, name="stat_t", tag="L")
+        nc.tensor.transpose(stat_t[:], stat[:], ident[:])
+        stat_col = const.tile([P, 1], F32, name="stat_col")
+        nc.vector.tensor_reduce(out=stat_col[:], in_=stat_t[:], axis=AX.X, op=ALU.max)
+        stat_all = ps_l.tile([P, P], F32, name="stat_all", tag="L")
+        nc.tensor.transpose(stat_all[:], stat_col[:, 0:1].to_broadcast([P, P]), ident[:])
+        mxmn = const.tile([P, 2 * D], F32, name="mxmn")
+        nc.vector.tensor_copy(out=mxmn[:], in_=stat_all[:, 0 : 2 * D])
+        span = const.tile([P, D], F32, name="span")
+        nc.vector.tensor_tensor(
+            out=span[:], in0=mxmn[:, 0:D], in1=mxmn[:, D : 2 * D], op=ALU.add
+        )
+        inv = const.tile([P, D], F32, name="inv")
+        nc.vector.reciprocal(inv[:], span[:])
+        xs = const.tile([P, NT, D], F32, name="xs")
+        nc.vector.tensor_tensor(
+            out=xs[:],
+            in0=xb[:],
+            in1=mxmn[:, D : 2 * D].unsqueeze(1).to_broadcast([P, NT, D]),
+            op=ALU.add,
+        )
+        nc.vector.tensor_tensor(
+            out=xs[:], in0=xs[:], in1=inv[:].unsqueeze(1).to_broadcast([P, NT, D]), op=ALU.mult
+        )
+        nhx = const.tile([P, NT, D], F32, name="nhx")
+        nc.vector.tensor_scalar(
+            out=nhx[:], in0=xs[:], scalar1=-0.5, scalar2=None, op0=ALU.mult
+        )
+
+        zf = const.tile([P, PASSES, PACK, D], F32, name="zf")
+        nc.vector.tensor_copy(out=zf[:], in_=zb[:])
+        zt = const.tile([P, D, M], F32, name="zt")
+        ks = sorted(set([config(j)[0] + config(j)[1] for j in range(NT)]))
+        hz = {}
+        cx = {}
+        flip = [0]
+
+        def leave_bank(dst, src):
+            if flip[0] % 2 == 0:
+                nc.scalar.copy(out=dst, in_=src)
+            else:
+                nc.vector.tensor_copy(out=dst, in_=src)
+            flip[0] += 1
+
+        def spread(dst, col_of):
+            for g in range(PASSES):
+                bank = ps_o.tile([P, PACK, P], F32, name="bank", tag="O")
+                for t in range(PACK):
+                    nc.tensor.transpose(
+                        bank[:, t, :], col_of(g, t).to_broadcast([P, P]), ident[:]
+                    )
+                leave_bank(
+                    dst[:, g * HALF : (g + 1) * HALF], bank[:].rearrange("p t n -> p (t n)")
+                )
+
+        for k in ks:
+            hsum = const.tile([P, PASSES, PACK], F32, name="hsum%d" % k)
+            nc.vector.tensor_reduce(out=hsum[:], in_=zf[:, :, :, 0:k], axis=AX.X, op=ALU.add)
+            hneg = const.tile([P, PASSES, PACK], F32, name="hneg%d" % k)
+            nc.vector.tensor_scalar(
+                out=hneg[:], in0=hsum[:], scalar1=-0.5, scalar2=None, op0=ALU.mult
+            )
+            hz[k] = const.tile([P, M], F32, name="hz%d" % k)
+            spread(hz[k], lambda g, t, h=hneg: h[:, g, t : t + 1])
+            cx[k] = const.tile([P, NT], F32, name="cx%d" % k)
+            nc.vector.tensor_reduce(out=cx[k][:], in_=nhx[:, :, 0:k], axis=AX.X, op=ALU.add)
+        for d in range(D):
+            spread(zt[:, d, :], lambda g, t, dd=d: zf[:, g, t, dd : dd + 1])
+
+        cgrp = const.tile([P, PASSES, COLS, PACK], BF16, name="cgrp", align_bytes=64)
+        c_codes = const.tile([P, PASSES, COLS], U32, name="c_codes", align_bytes=64)
+        c_scales = const.tile([P, PASSES, COLS], U8, name="c_scales", align_bytes=64)
+        for g in range(PASSES):
+            nc.vector.tensor_copy(
+                out=cgrp[:, g].rearrange("p (c i) t -> p c t i", i=4),
+                in_=craw[:, g].rearrange("p t (c i) -> p c t i", i=4),
+            )
+        for g in range(PASSES):
+            nc.vector.quantize_mx(
+                out=c_codes[:, g, :].bitcast(FP8X4),
+                scales=c_scales[:, g, :],
+                in_=cgrp[:, g].rearrange("p c t -> p (c t)"),
+            )
+
+        out_view = out.rearrange("(p j) c -> j p c", j=NT)
+        terms = {}
+        banks = {}
+        groups = {}
+        quant = {}
+        sums = {}
+
+        def stage_terms(j):
+            n_chain, n_leaf, n_abs = config(j)
+            k = n_chain + n_leaf
+            made = []
+            for i in range(n_abs):
+                d = k + i
+                leaf = terms_pool.tile([P, M], F32, name="abs%d" % i)
+                nc.scalar.activation(
+                    out=leaf[:],
+                    in_=zt[:, d, :],
+                    func=ACTF.Abs,
+                    bias=nhx[:, j, d : d + 1],
+                    scale=0.5,
+                )
+                made.append(leaf)
+            acc = terms_pool.tile([P, M], F32, name="acc")
+            for i in range(max(n_chain, n_leaf)):
+                if i < n_chain:
+                    nc.vector.scalar_tensor_tensor(
+                        out=acc[:],
+                        in0=zt[:, i, :],
+                        scalar=xs[:, j, i : i + 1],
+                        in1=(hz[k][:] if i == 0 else acc[:]),
+                        op0=ALU.max,
+                        op1=ALU.add,
+                    )
+                if i < n_leaf:
+                    d = n_chain + i
+                    leaf = terms_pool.tile([P, M], F32, name="max%d" % i)
+                    if i == 0:
+                        nc.vector.tensor_scalar(
+                            out=leaf[:],
+                            in0=zt[:, d, :],
+                            scalar1=xs[:, j, d : d + 1],
+                            scalar2=cx[k][:, j : j + 1],
+                            op0=ALU.max,
+                            op1=ALU.add,
+                        )
+                    else:
+                        nc.vector.tensor_scalar(
+                            out=leaf[:],
+                            in0=zt[:, d, :],
+                            scalar1=xs[:, j, d : d + 1],
+                            scalar2=None,
+                            op0=ALU.max,
+                        )
+                    made.append(leaf)
+            made.append(acc)
+            terms[j] = made
+
+        def stage_sum(j):
+            made = terms[j]
+            banks[j] = []
+            for g in range(PASSES):
+                bank = ps_l.tile([P, PACK, P], F32, name="l1t", tag="L")
+                for t in range(PACK):
+                    b = PACK * g + t
+                    for i, term in enumerate(made):
+                        nc.tensor.matmul(
+                            bank[:, t, :],
+                            lhsT=term[:, b * P : (b + 1) * P],
+                            rhs=ident[:],
+                            is_transpose=True,
+                            start=(i == 0),
+                            stop=(i == len(made) - 1),
+                        )
+                banks[j].append(bank)
+
+        def stage_exp(j):
+            grp = work.tile([P, PASSES, P, PACK], BF16, name="grp", align_bytes=64)
+            for g, bank in enumerate(banks[j]):
+                nc.scalar.activation(
+                    out=grp[:, g],
+                    in_=bank[:].rearrange("p t n -> p n t"),
+                    func=ACTF.Exp,
+                    scale=-2.0,
+                )
+            groups[j] = grp
+
+        def stage_quant(j):
+            grp = groups[j]
+            codes = work.tile([P, PASSES * P], U32, name="codes", align_bytes=64)
+            scales = work.tile([P, PASSES * P], U8, name="scales", align_bytes=64)
+            nc.vector.quantize_mx(
+                out=codes[:].bitcast(FP8X4),
+                scales=scales[:],
+                in_=grp[:].rearrange("p g n t -> p (g n t)"),
+            )
+            quant[j] = (codes, scales)
+
+        def stage_mx(j):
+            codes, scales = quant[j]
+            sums[j] = []
+            for h in range(COLS // HALF):
+                acc = ps_o.tile([P, HALF], F32, name="osum", tag="O")
+                for g in range(PASSES):
+                    nc.tensor.matmul_mx(
+                        out=acc[:],
+                        lhsT=codes[:, g * P : (g + 1) * P].bitcast(FP8X4),
+                        lhsT_scale=scales[:, g * P : (g + 1) * P],
+                        rhs=c_codes[:, g, h * HALF : (h + 1) * HALF].bitcast(FP8X4),
+                        rhs_scale=c_scales[:, g, h * HALF : (h + 1) * HALF],
+                        start=(g == 0),
+                        stop=(g == PASSES - 1),
+                    )
+                sums[j].append(acc)
+
+        def stage_store(j):
+            res = work.tile([P, COLS], F32, name="res")
+            for h, acc in enumerate(sums[j]):
+                nc.scalar.copy(out=res[:, h * HALF : (h + 1) * HALF], in_=acc[:])
+            nc.sync.dma_start(out=out_view[j], in_=res[:])
+
+        for i in range(NT + 5):
+            if 0 <= i - 3 < NT:
+                stage_quant(i - 3)
+            if 0 <= i - 2 < NT:
+                stage_exp(i - 2)
+            if 0 <= i - 5 < NT:
+                stage_store(i - 5)
+            if 0 <= i - 4 < NT:
+                stage_mx(i - 4)
+            if i < NT:
+                stage_terms(i)
+            if 0 <= i - 1 < NT:
+                stage_sum(i - 1)

@@ -51,6 +51,10 @@ def tile_tmgp_sg_kernel(tc, x, design_points, chol_inv, out):
 
         ident = const.tile([P, P], F32, name="ident")
         make_identity(nc, ident[:])
+        warm_in = const.tile([P, 1], F32, name="warm_in")
+        warm_out = const.tile([P, 1], F32, name="warm_out")
+        nc.vector.memset(warm_in[:], 0.0)
+        nc.scalar.activation(out=warm_out[:], in_=warm_in[:], func=ACTF.Exp)
 
         stat = const.tile([P, P], F32, name="stat")
         nc.vector.memset(stat[:], 0.0)
@@ -127,18 +131,22 @@ def tile_tmgp_sg_kernel(tc, x, design_points, chol_inv, out):
             spread(hz[k], lambda g, t, h=hneg: h[:, g, t : t + 1])
             cx[k] = const.tile([P, NT], F32, name="cx%d" % k)
             nc.vector.tensor_reduce(out=cx[k][:], in_=nhx[:, :, 0:k], axis=AX.X, op=ALU.add)
-        for d in range(D):
+        for d in (0, 3, 6, 1, 4, 7, 2, 5):
             spread(zt[:, d, :], lambda g, t, dd=d: zf[:, g, t, dd : dd + 1])
 
         cgrp = const.tile([P, PASSES, COLS, PACK], BF16, name="cgrp", align_bytes=64)
         c_codes = const.tile([P, PASSES, COLS], U32, name="c_codes", align_bytes=64)
         c_scales = const.tile([P, PASSES, COLS], U8, name="c_scales", align_bytes=64)
-        for g in range(PASSES):
-            nc.vector.tensor_copy(
-                out=cgrp[:, g].rearrange("p (c i) t -> p c t i", i=4),
-                in_=craw[:, g].rearrange("p t (c i) -> p c t i", i=4),
+
+        def regroup_c(piece):
+            g, h = divmod(piece, 2)
+            cols = slice(h * HALF, (h + 1) * HALF)
+            nc.scalar.copy(
+                out=cgrp[:, g, cols, :].rearrange("p (c i) t -> p c t i", i=4),
+                in_=craw[:, g, :, cols].rearrange("p t (c i) -> p c t i", i=4),
             )
-        for g in range(PASSES):
+
+        def quantise_c(g):
             nc.vector.quantize_mx(
                 out=c_codes[:, g, :].bitcast(FP8X4),
                 scales=c_scales[:, g, :],
@@ -202,10 +210,11 @@ def tile_tmgp_sg_kernel(tc, x, design_points, chol_inv, out):
             made.append(acc)
             terms[j] = made
 
-        def stage_sum(j):
+        def stage_sum(j, g):
             made = terms[j]
-            banks[j] = []
-            for g in range(PASSES):
+            if g == 0:
+                banks[j] = []
+            if True:
                 bank = ps_l.tile([P, PACK, P], F32, name="l1t", tag="L")
                 for t in range(PACK):
                     b = PACK * g + t
@@ -242,10 +251,11 @@ def tile_tmgp_sg_kernel(tc, x, design_points, chol_inv, out):
             )
             quant[j] = (codes, scales)
 
-        def stage_mx(j):
+        def stage_mx(j, h):
             codes, scales = quant[j]
-            sums[j] = []
-            for h in range(COLS // HALF):
+            if h == 0:
+                sums[j] = []
+            if True:
                 acc = ps_o.tile([P, HALF], F32, name="osum", tag="O")
                 for g in range(PASSES):
                     nc.tensor.matmul_mx(
@@ -265,16 +275,23 @@ def tile_tmgp_sg_kernel(tc, x, design_points, chol_inv, out):
                 nc.scalar.copy(out=res[:, h * HALF : (h + 1) * HALF], in_=acc[:])
             nc.sync.dma_start(out=out_view[j], in_=res[:])
 
-        for i in range(NT + 5):
-            if 0 <= i - 3 < NT:
-                stage_quant(i - 3)
-            if 0 <= i - 2 < NT:
-                stage_exp(i - 2)
-            if 0 <= i - 5 < NT:
-                stage_store(i - 5)
-            if 0 <= i - 4 < NT:
-                stage_mx(i - 4)
-            if i < NT:
-                stage_terms(i)
-            if 0 <= i - 1 < NT:
-                stage_sum(i - 1)
+        with tc.manual_schedule():
+            for i in range(NT + 5):
+                if i == 4:
+                    quantise_c(0)
+                    quantise_c(1)
+                if 0 <= i - 3 < NT:
+                    stage_quant(i - 3)
+                if 0 <= i - 2 < NT:
+                    stage_exp(i - 2)
+                if 0 <= i - 5 < NT:
+                    stage_store(i - 5)
+                if i < NT:
+                    stage_terms(i)
+                if i < 4:
+                    regroup_c(i)
+                for half in range(2):
+                    if 0 <= i - 1 < NT:
+                        stage_sum(i - 1, half)
+                    if 0 <= i - 4 < NT:
+                        stage_mx(i - 4, half)

@@ -24,15 +24,15 @@ HALF = 512
 FLOPS = 2 * N_ROWS * M * COLS
 
 
-def config(j):
-    return (3, 3, 2)
+def n_chain_of(j):
+    return 5 if j % 4 == 3 else 4
 
 
 def tile_tmgp_sg_kernel(tc, x, design_points, chol_inv, out):
     nc = tc.nc
     with ExitStack() as ctx:
         const = ctx.enter_context(tc.tile_pool(name="const", bufs=1))
-        terms_pool = ctx.enter_context(tc.tile_pool(name="terms", bufs=3))
+        terms_pool = ctx.enter_context(tc.tile_pool(name="terms", bufs=4))
         work = ctx.enter_context(tc.tile_pool(name="work", bufs=3))
         ps_l = ctx.enter_context(tc.psum_pool(name="ps_l", bufs=4))
         ps_o = ctx.enter_context(tc.psum_pool(name="ps_o", bufs=4))
@@ -97,7 +97,6 @@ def tile_tmgp_sg_kernel(tc, x, design_points, chol_inv, out):
         zf = const.tile([P, PASSES, PACK, D], F32, name="zf")
         nc.vector.tensor_copy(out=zf[:], in_=zb[:])
         zt = const.tile([P, D, M], F32, name="zt")
-        ks = sorted(set([config(j)[0] + config(j)[1] for j in range(NT)]))
         hz = {}
         cx = {}
         flip = [0]
@@ -120,7 +119,10 @@ def tile_tmgp_sg_kernel(tc, x, design_points, chol_inv, out):
                     dst[:, g * HALF : (g + 1) * HALF], bank[:].rearrange("p t n -> p (t n)")
                 )
 
-        for k in ks:
+        def spread_dim(d):
+            spread(zt[:, d, :], lambda g, t: zf[:, g, t, d : d + 1])
+
+        def spread_half_sums(k):
             hsum = const.tile([P, PASSES, PACK], F32, name="hsum%d" % k)
             nc.vector.tensor_reduce(out=hsum[:], in_=zf[:, :, :, 0:k], axis=AX.X, op=ALU.add)
             hneg = const.tile([P, PASSES, PACK], F32, name="hneg%d" % k)
@@ -128,11 +130,14 @@ def tile_tmgp_sg_kernel(tc, x, design_points, chol_inv, out):
                 out=hneg[:], in0=hsum[:], scalar1=-0.5, scalar2=None, op0=ALU.mult
             )
             hz[k] = const.tile([P, M], F32, name="hz%d" % k)
-            spread(hz[k], lambda g, t, h=hneg: h[:, g, t : t + 1])
+            spread(hz[k], lambda g, t: hneg[:, g, t : t + 1])
             cx[k] = const.tile([P, NT], F32, name="cx%d" % k)
             nc.vector.tensor_reduce(out=cx[k][:], in_=nhx[:, :, 0:k], axis=AX.X, op=ALU.add)
-        for d in (0, 3, 6, 1, 4, 7, 2, 5):
-            spread(zt[:, d, :], lambda g, t, dd=d: zf[:, g, t, dd : dd + 1])
+
+        spread_half_sums(5)
+        for d in (0, 5, 4, 1, 6, 2, 7, 3):
+            spread_dim(d)
+        spread_half_sums(6)
 
         cgrp = const.tile([P, PASSES, COLS, PACK], BF16, name="cgrp", align_bytes=64)
         c_codes = const.tile([P, PASSES, COLS], U32, name="c_codes", align_bytes=64)
@@ -161,12 +166,11 @@ def tile_tmgp_sg_kernel(tc, x, design_points, chol_inv, out):
         sums = {}
 
         def stage_terms(j):
-            n_chain, n_leaf, n_abs = config(j)
-            k = n_chain + n_leaf
-            made = []
-            for i in range(n_abs):
-                d = k + i
-                leaf = terms_pool.tile([P, M], F32, name="abs%d" % i)
+            n_chain = n_chain_of(j)
+            k = n_chain + 1
+            abs_leaves = []
+            for d in range(k, D):
+                leaf = terms_pool.tile([P, M], F32, name="abs%d" % (d - k))
                 nc.scalar.activation(
                     out=leaf[:],
                     in_=zt[:, d, :],
@@ -174,60 +178,51 @@ def tile_tmgp_sg_kernel(tc, x, design_points, chol_inv, out):
                     bias=nhx[:, j, d : d + 1],
                     scale=0.5,
                 )
-                made.append(leaf)
+                abs_leaves.append(leaf)
             acc = terms_pool.tile([P, M], F32, name="acc")
-            for i in range(max(n_chain, n_leaf)):
-                if i < n_chain:
+            max_leaf = terms_pool.tile([P, M], F32, name="max_leaf")
+            for d in range(n_chain):
+                for h in range(2):
+                    cols = slice(h * HALF, (h + 1) * HALF)
                     nc.vector.scalar_tensor_tensor(
-                        out=acc[:],
-                        in0=zt[:, i, :],
-                        scalar=xs[:, j, i : i + 1],
-                        in1=(hz[k][:] if i == 0 else acc[:]),
+                        out=acc[:, cols],
+                        in0=zt[:, d, cols],
+                        scalar=xs[:, j, d : d + 1],
+                        in1=(hz[k][:, cols] if d == 0 else acc[:, cols]),
                         op0=ALU.max,
                         op1=ALU.add,
                     )
-                if i < n_leaf:
-                    d = n_chain + i
-                    leaf = terms_pool.tile([P, M], F32, name="max%d" % i)
-                    if i == 0:
-                        nc.vector.tensor_scalar(
-                            out=leaf[:],
-                            in0=zt[:, d, :],
-                            scalar1=xs[:, j, d : d + 1],
-                            scalar2=cx[k][:, j : j + 1],
-                            op0=ALU.max,
-                            op1=ALU.add,
-                        )
-                    else:
-                        nc.vector.tensor_scalar(
-                            out=leaf[:],
-                            in0=zt[:, d, :],
-                            scalar1=xs[:, j, d : d + 1],
-                            scalar2=None,
-                            op0=ALU.max,
-                        )
-                    made.append(leaf)
-            made.append(acc)
-            terms[j] = made
+                if d == 0:
+                    nc.vector.tensor_scalar(
+                        out=max_leaf[:],
+                        in0=zt[:, n_chain, :],
+                        scalar1=xs[:, j, n_chain : n_chain + 1],
+                        scalar2=cx[k][:, j : j + 1],
+                        op0=ALU.max,
+                        op1=ALU.add,
+                    )
+            terms[j] = abs_leaves[:1] + [max_leaf] + abs_leaves[1:] + [acc]
 
-        def stage_sum(j, g):
+        def stage_sum(j):
             made = terms[j]
-            if g == 0:
-                banks[j] = []
-            if True:
+            last = len(made) - 1
+            pair = []
+            for g in range(PASSES):
                 bank = ps_l.tile([P, PACK, P], F32, name="l1t", tag="L")
-                for t in range(PACK):
-                    b = PACK * g + t
-                    for i, term in enumerate(made):
+                pair.append(bank)
+            for i, term in enumerate(made):
+                for g in range(PASSES):
+                    for t in range(PACK):
+                        b = PACK * g + t
                         nc.tensor.matmul(
-                            bank[:, t, :],
+                            pair[g][:, t, :],
                             lhsT=term[:, b * P : (b + 1) * P],
                             rhs=ident[:],
                             is_transpose=True,
-                            start=(i == 0),
-                            stop=(i == len(made) - 1),
+                            start=(i == 0 and t == 0),
+                            stop=(i == last and t == PACK - 1),
                         )
-                banks[j].append(bank)
+            banks[j] = pair
 
         def stage_exp(j):
             grp = work.tile([P, PASSES, P, PACK], BF16, name="grp", align_bytes=64)
@@ -242,8 +237,8 @@ def tile_tmgp_sg_kernel(tc, x, design_points, chol_inv, out):
 
         def stage_quant(j):
             grp = groups[j]
-            codes = work.tile([P, PASSES * P], U32, name="codes", align_bytes=64)
-            scales = work.tile([P, PASSES * P], U8, name="scales", align_bytes=64)
+            codes = work.tile([P, PASSES * P], U32, name="codes", align_bytes=64, bufs=4)
+            scales = work.tile([P, PASSES * P], U8, name="scales", align_bytes=64, bufs=4)
             nc.vector.quantize_mx(
                 out=codes[:].bitcast(FP8X4),
                 scales=scales[:],
@@ -251,11 +246,10 @@ def tile_tmgp_sg_kernel(tc, x, design_points, chol_inv, out):
             )
             quant[j] = (codes, scales)
 
-        def stage_mx(j, h):
+        def stage_mx(j):
             codes, scales = quant[j]
-            if h == 0:
-                sums[j] = []
-            if True:
+            sums[j] = []
+            for h in range(COLS // HALF):
                 acc = ps_o.tile([P, HALF], F32, name="osum", tag="O")
                 for g in range(PASSES):
                     nc.tensor.matmul_mx(
@@ -276,22 +270,22 @@ def tile_tmgp_sg_kernel(tc, x, design_points, chol_inv, out):
             nc.sync.dma_start(out=out_view[j], in_=res[:])
 
         with tc.manual_schedule():
-            for i in range(NT + 5):
-                if i == 4:
-                    quantise_c(0)
-                    quantise_c(1)
+            for i in range(NT + 6):
                 if 0 <= i - 3 < NT:
                     stage_quant(i - 3)
                 if 0 <= i - 2 < NT:
                     stage_exp(i - 2)
-                if 0 <= i - 5 < NT:
-                    stage_store(i - 5)
+                if 0 <= i - 6 < NT:
+                    stage_store(i - 6)
                 if i < NT:
                     stage_terms(i)
                 if i < 4:
                     regroup_c(i)
-                for half in range(2):
-                    if 0 <= i - 1 < NT:
-                        stage_sum(i - 1, half)
-                    if 0 <= i - 4 < NT:
-                        stage_mx(i - 4, half)
+                if i == 4:
+                    quantise_c(0)
+                    quantise_c(1)
+                if 0 <= i - 1 < NT:
+                    stage_sum(i - 1)
+                if i % 2 == 1 and 0 <= i - 5 < NT:
+                    stage_mx(i - 5)
+                    stage_mx(i - 4)

@@ -25,7 +25,7 @@ FLOPS = 2 * N_ROWS * M * COLS
 
 
 def n_chain_of(j):
-    return 5 if j % 4 == 3 else 4
+    return 5 if (j > 0 and j % 7 == 0) else 4
 
 
 def tile_tmgp_sg_kernel(tc, x, design_points, chol_inv, out):
@@ -51,6 +51,8 @@ def tile_tmgp_sg_kernel(tc, x, design_points, chol_inv, out):
 
         ident = const.tile([P, P], F32, name="ident")
         make_identity(nc, ident[:])
+        ident_bf = const.tile([P, P], BF16, name="ident_bf")
+        make_identity(nc, ident_bf[:])
         warm_in = const.tile([P, 1], F32, name="warm_in")
         warm_out = const.tile([P, 1], F32, name="warm_out")
         nc.vector.memset(warm_in[:], 0.0)
@@ -108,19 +110,19 @@ def tile_tmgp_sg_kernel(tc, x, design_points, chol_inv, out):
                 nc.vector.tensor_copy(out=dst, in_=src)
             flip[0] += 1
 
-        def spread(dst, col_of):
+        def spread(dst, col_of, dtype, eye):
             for g in range(PASSES):
-                bank = ps_o.tile([P, PACK, P], F32, name="bank", tag="O")
+                bank = ps_o.tile([P, PACK, P], dtype, name="bank", tag="O")
                 for t in range(PACK):
                     nc.tensor.transpose(
-                        bank[:, t, :], col_of(g, t).to_broadcast([P, P]), ident[:]
+                        bank[:, t, :], col_of(g, t).to_broadcast([P, P]), eye[:]
                     )
                 leave_bank(
                     dst[:, g * HALF : (g + 1) * HALF], bank[:].rearrange("p t n -> p (t n)")
                 )
 
         def spread_dim(d):
-            spread(zt[:, d, :], lambda g, t: zf[:, g, t, d : d + 1])
+            spread(zt[:, d, :], lambda g, t: zb[:, g, t, d : d + 1], BF16, ident_bf)
 
         def spread_half_sums(k):
             hsum = const.tile([P, PASSES, PACK], F32, name="hsum%d" % k)
@@ -130,7 +132,7 @@ def tile_tmgp_sg_kernel(tc, x, design_points, chol_inv, out):
                 out=hneg[:], in0=hsum[:], scalar1=-0.5, scalar2=None, op0=ALU.mult
             )
             hz[k] = const.tile([P, M], F32, name="hz%d" % k)
-            spread(hz[k], lambda g, t: hneg[:, g, t : t + 1])
+            spread(hz[k], lambda g, t: hneg[:, g, t : t + 1], F32, ident)
             cx[k] = const.tile([P, NT], F32, name="cx%d" % k)
             nc.vector.tensor_reduce(out=cx[k][:], in_=nhx[:, :, 0:k], axis=AX.X, op=ALU.add)
 
@@ -182,8 +184,7 @@ def tile_tmgp_sg_kernel(tc, x, design_points, chol_inv, out):
             acc = terms_pool.tile([P, M], F32, name="acc")
             max_leaf = terms_pool.tile([P, M], F32, name="max_leaf")
             for d in range(n_chain):
-                for h in range(2):
-                    cols = slice(h * HALF, (h + 1) * HALF)
+                for cols in ([slice(0, M)] if d == 0 else [slice(0, HALF), slice(HALF, M)]):
                     nc.vector.scalar_tensor_tensor(
                         out=acc[:, cols],
                         in0=zt[:, d, cols],
@@ -266,26 +267,35 @@ def tile_tmgp_sg_kernel(tc, x, design_points, chol_inv, out):
         def stage_store(j):
             res = work.tile([P, COLS], F32, name="res")
             for h, acc in enumerate(sums[j]):
-                nc.scalar.copy(out=res[:, h * HALF : (h + 1) * HALF], in_=acc[:])
-            nc.sync.dma_start(out=out_view[j], in_=res[:])
+                cols = slice(h * HALF, (h + 1) * HALF)
+                if j >= NT - 2 and h == 1:
+                    nc.vector.tensor_copy(out=res[:, cols], in_=acc[:])
+                else:
+                    nc.scalar.copy(out=res[:, cols], in_=acc[:])
+                if j == NT - 1:
+                    nc.sync.dma_start(out=out_view[j][:, cols], in_=res[:, cols])
+            if j < NT - 1:
+                nc.sync.dma_start(out=out_view[j], in_=res[:])
 
         with tc.manual_schedule():
-            for i in range(NT + 6):
+            for i in range(NT + 5):
                 if 0 <= i - 3 < NT:
                     stage_quant(i - 3)
                 if 0 <= i - 2 < NT:
                     stage_exp(i - 2)
-                if 0 <= i - 6 < NT:
-                    stage_store(i - 6)
+                if 0 <= i - 5 < NT:
+                    stage_store(i - 5)
                 if i < NT:
                     stage_terms(i)
-                if i < 4:
-                    regroup_c(i)
-                if i == 4:
+                if i == 0:
+                    regroup_c(0)
+                if i < 3:
+                    regroup_c(i + 1)
+                if i == 3:
                     quantise_c(0)
                     quantise_c(1)
                 if 0 <= i - 1 < NT:
                     stage_sum(i - 1)
-                if i % 2 == 1 and 0 <= i - 5 < NT:
-                    stage_mx(i - 5)
+                if i % 2 == 0 and 0 <= i - 4 < NT:
                     stage_mx(i - 4)
+                    stage_mx(i - 3)

@@ -24,8 +24,11 @@ HALF = 512
 FLOPS = 2 * N_ROWS * M * COLS
 
 
-def n_chain_of(j):
-    return 5 if (j > 0 and j % 7 == 0) else 4
+N_LEAF = 2
+
+
+def n_abs_of(j):
+    return 2 if j % 8 in (2, 5, 7) else 3
 
 
 def tile_tmgp_sg_kernel(tc, x, design_points, chol_inv, out):
@@ -168,8 +171,8 @@ def tile_tmgp_sg_kernel(tc, x, design_points, chol_inv, out):
         sums = {}
 
         def stage_terms(j):
-            n_chain = n_chain_of(j)
-            k = n_chain + 1
+            k = D - n_abs_of(j)
+            n_chain = k - N_LEAF
             abs_leaves = []
             for d in range(k, D):
                 leaf = terms_pool.tile([P, M], F32, name="abs%d" % (d - k))
@@ -182,7 +185,7 @@ def tile_tmgp_sg_kernel(tc, x, design_points, chol_inv, out):
                 )
                 abs_leaves.append(leaf)
             acc = terms_pool.tile([P, M], F32, name="acc")
-            max_leaf = terms_pool.tile([P, M], F32, name="max_leaf")
+            max_leaves = []
             for d in range(n_chain):
                 for cols in ([slice(0, M)] if d == 0 else [slice(0, HALF), slice(HALF, M)]):
                     nc.vector.scalar_tensor_tensor(
@@ -193,16 +196,28 @@ def tile_tmgp_sg_kernel(tc, x, design_points, chol_inv, out):
                         op0=ALU.max,
                         op1=ALU.add,
                     )
-                if d == 0:
-                    nc.vector.tensor_scalar(
-                        out=max_leaf[:],
-                        in0=zt[:, n_chain, :],
-                        scalar1=xs[:, j, n_chain : n_chain + 1],
-                        scalar2=cx[k][:, j : j + 1],
-                        op0=ALU.max,
-                        op1=ALU.add,
-                    )
-            terms[j] = abs_leaves[:1] + [max_leaf] + abs_leaves[1:] + [acc]
+                if d < N_LEAF:
+                    e = n_chain + d
+                    max_leaf = terms_pool.tile([P, M], F32, name="max_leaf%d" % d)
+                    if d == 0:
+                        nc.vector.tensor_scalar(
+                            out=max_leaf[:],
+                            in0=zt[:, e, :],
+                            scalar1=xs[:, j, e : e + 1],
+                            scalar2=cx[k][:, j : j + 1],
+                            op0=ALU.max,
+                            op1=ALU.add,
+                        )
+                    else:
+                        nc.vector.tensor_scalar(
+                            out=max_leaf[:],
+                            in0=zt[:, e, :],
+                            scalar1=xs[:, j, e : e + 1],
+                            scalar2=None,
+                            op0=ALU.max,
+                        )
+                    max_leaves.append(max_leaf)
+            terms[j] = abs_leaves[:1] + max_leaves[:1] + abs_leaves[1:] + max_leaves[1:] + [acc]
 
         def stage_sum(j):
             made = terms[j]

@@ -101,7 +101,7 @@ def tile_tmgp_sg_kernel(tc, x, design_points, chol_inv, out):
 
         zf = const.tile([P, PASSES, PACK, D], F32, name="zf")
         nc.vector.tensor_copy(out=zf[:], in_=zb[:])
-        zt = const.tile([P, D, M], F32, name="zt")
+        zt = const.tile([P, D, M], BF16, name="zt")
         hz = {}
         cx = {}
         flip = [0]
@@ -125,7 +125,15 @@ def tile_tmgp_sg_kernel(tc, x, design_points, chol_inv, out):
                 )
 
         def spread_dim(d):
-            spread(zt[:, d, :], lambda g, t: zb[:, g, t, d : d + 1], BF16, ident_bf)
+            bank = ps_o.tile([P, PASSES * PACK, P], BF16, name="zbank", tag="O")
+            for g in range(PASSES):
+                for t in range(PACK):
+                    nc.tensor.transpose(
+                        bank[:, PACK * g + t, :],
+                        zb[:, g, t, d : d + 1].to_broadcast([P, P]),
+                        ident_bf[:],
+                    )
+            leave_bank(zt[:, d, :], bank[:].rearrange("p b n -> p (b n)"))
 
         def spread_half_sums(k):
             hsum = const.tile([P, PASSES, PACK], F32, name="hsum%d" % k)
@@ -187,15 +195,16 @@ def tile_tmgp_sg_kernel(tc, x, design_points, chol_inv, out):
             acc = terms_pool.tile([P, M], F32, name="acc")
             max_leaves = []
             for d in range(n_chain):
-                for cols in ([slice(0, M)] if d == 0 else [slice(0, HALF), slice(HALF, M)]):
-                    nc.vector.scalar_tensor_tensor(
-                        out=acc[:, cols],
-                        in0=zt[:, d, cols],
-                        scalar=xs[:, j, d : d + 1],
-                        in1=(hz[k][:, cols] if d == 0 else acc[:, cols]),
-                        op0=ALU.max,
-                        op1=ALU.add,
-                    )
+                if d == N_LEAF + 1 and 0 <= j - 3:
+                    stage_quant(j - 3)
+                nc.vector.scalar_tensor_tensor(
+                    out=acc[:],
+                    in0=zt[:, d, :],
+                    scalar=xs[:, j, d : d + 1],
+                    in1=(hz[k][:] if d == 0 else acc[:]),
+                    op0=ALU.max,
+                    op1=ALU.add,
+                )
                 if d < N_LEAF:
                     e = n_chain + d
                     max_leaf = terms_pool.tile([P, M], F32, name="max_leaf%d" % d)
@@ -294,7 +303,7 @@ def tile_tmgp_sg_kernel(tc, x, design_points, chol_inv, out):
 
         with tc.manual_schedule():
             for i in range(NT + 5):
-                if 0 <= i - 3 < NT:
+                if 0 <= i - 3 < NT and not (i < NT and n_abs_of(i) == 2):
                     stage_quant(i - 3)
                 if 0 <= i - 2 < NT:
                     stage_exp(i - 2)

@@ -24,11 +24,12 @@ HALF = 512
 FLOPS = 2 * N_ROWS * M * COLS
 
 
-N_LEAF = 2
-
-
 def n_abs_of(j):
-    return 2 if j % 8 in (2, 5, 7) else 3
+    return 2 if j % 2 == 1 else 3
+
+
+def n_chain_of(j):
+    return 4 if j % 6 == 1 else 3
 
 
 def tile_tmgp_sg_kernel(tc, x, design_points, chol_inv, out):
@@ -180,7 +181,8 @@ def tile_tmgp_sg_kernel(tc, x, design_points, chol_inv, out):
 
         def stage_terms(j):
             k = D - n_abs_of(j)
-            n_chain = k - N_LEAF
+            n_chain = n_chain_of(j)
+            n_leaf = k - n_chain
             abs_leaves = []
             for d in range(k, D):
                 leaf = terms_pool.tile([P, M], F32, name="abs%d" % (d - k))
@@ -195,7 +197,7 @@ def tile_tmgp_sg_kernel(tc, x, design_points, chol_inv, out):
             acc = terms_pool.tile([P, M], F32, name="acc")
             max_leaves = []
             for d in range(n_chain):
-                if d == N_LEAF + 1 and 0 <= j - 3:
+                if d == 3 and 0 <= j - 3:
                     stage_quant(j - 3)
                 nc.vector.scalar_tensor_tensor(
                     out=acc[:],
@@ -205,7 +207,7 @@ def tile_tmgp_sg_kernel(tc, x, design_points, chol_inv, out):
                     op0=ALU.max,
                     op1=ALU.add,
                 )
-                if d < N_LEAF:
+                if d < n_leaf:
                     e = n_chain + d
                     max_leaf = terms_pool.tile([P, M], F32, name="max_leaf%d" % d)
                     if d == 0:
@@ -303,7 +305,7 @@ def tile_tmgp_sg_kernel(tc, x, design_points, chol_inv, out):
 
         with tc.manual_schedule():
             for i in range(NT + 5):
-                if 0 <= i - 3 < NT and not (i < NT and n_abs_of(i) == 2):
+                if 0 <= i - 3 < NT and not (i < NT and n_chain_of(i) == 4):
                     stage_quant(i - 3)
                 if 0 <= i - 2 < NT:
                     stage_exp(i - 2)

@@ -29,7 +29,9 @@ def n_abs_of(j):
 
 
 def n_chain_of(j):
-    return 4 if j % 6 == 1 else 3
+    if j % 2 == 1:
+        return 4
+    return 3 if j % 6 == 0 else 2
 
 
 def tile_tmgp_sg_kernel(tc, x, design_points, chol_inv, out):
@@ -196,17 +198,18 @@ def tile_tmgp_sg_kernel(tc, x, design_points, chol_inv, out):
                 abs_leaves.append(leaf)
             acc = terms_pool.tile([P, M], F32, name="acc")
             max_leaves = []
-            for d in range(n_chain):
+            for d in range(max(n_chain, n_leaf)):
                 if d == 3 and 0 <= j - 3:
                     stage_quant(j - 3)
-                nc.vector.scalar_tensor_tensor(
-                    out=acc[:],
-                    in0=zt[:, d, :],
-                    scalar=xs[:, j, d : d + 1],
-                    in1=(hz[k][:] if d == 0 else acc[:]),
-                    op0=ALU.max,
-                    op1=ALU.add,
-                )
+                if d < n_chain:
+                    nc.vector.scalar_tensor_tensor(
+                        out=acc[:],
+                        in0=zt[:, d, :],
+                        scalar=xs[:, j, d : d + 1],
+                        in1=(hz[k][:] if d == 0 else acc[:]),
+                        op0=ALU.max,
+                        op1=ALU.add,
+                    )
                 if d < n_leaf:
                     e = n_chain + d
                     max_leaf = terms_pool.tile([P, M], F32, name="max_leaf%d" % d)
@@ -228,7 +231,7 @@ def tile_tmgp_sg_kernel(tc, x, design_points, chol_inv, out):
                             op0=ALU.max,
                         )
                     max_leaves.append(max_leaf)
-            terms[j] = abs_leaves[:1] + max_leaves[:1] + abs_leaves[1:] + max_leaves[1:] + [acc]
+            terms[j] = abs_leaves[:1] + max_leaves[:1] + abs_leaves[1:] + max_leaves[1:2] + [acc] + max_leaves[2:]
 
         def stage_sum(j):
             made = terms[j]

from contextlib import ExitStack

import concourse.mybir as mybir
from concourse.masks import make_identity

F32 = mybir.dt.float32
BF16 = mybir.dt.bfloat16
U32 = mybir.dt.uint32
U8 = mybir.dt.uint8
FP8X4 = mybir.dt.float8_e4m3fn_x4
ALU = mybir.AluOpType
ACTF = mybir.ActivationFunctionType
AX = mybir.AxisListType

P = 128
N_ROWS = 4096
D = 8
M = 1024
COLS = 1024
NT = N_ROWS // P
PACK = 4
PASSES = M // (P * PACK)
HALF = 512
FLOPS = 2 * N_ROWS * M * COLS


def n_abs_of(j):
    return 2 if j % 2 == 1 else 3


def n_chain_of(j):
    if j % 2 == 1:
        return 4
    return 3 if j % 6 == 0 else 2


def tile_tmgp_sg_kernel(tc, x, design_points, chol_inv, out):
    nc = tc.nc
    with ExitStack() as ctx:
        const = ctx.enter_context(tc.tile_pool(name="const", bufs=1))
        terms_pool = ctx.enter_context(tc.tile_pool(name="terms", bufs=4))
        work = ctx.enter_context(tc.tile_pool(name="work", bufs=3))
        ps_l = ctx.enter_context(tc.psum_pool(name="ps_l", bufs=4))
        ps_o = ctx.enter_context(tc.psum_pool(name="ps_o", bufs=4))

        xb = const.tile([P, NT, D], BF16, name="xb")
        nc.sync.dma_start(out=xb[:], in_=x.rearrange("(p j) d -> p j d", j=NT))
        zb = const.tile([P, PASSES, PACK, D], BF16, name="zb")
        nc.sync.dma_start(
            out=zb[:],
            in_=design_points.rearrange("(g p t) d -> p g t d", g=PASSES, t=PACK),
        )
        craw = const.tile([P, PASSES, PACK, COLS], BF16, name="craw")
        c_view = chol_inv.rearrange("(g p t) c -> g p t c", g=PASSES, t=PACK)
        for g in range(PASSES):
            nc.sync.dma_start(out=craw[:, g], in_=c_view[g])

        ident = const.tile([P, P], F32, name="ident")
        make_identity(nc, ident[:])
        ident_bf = const.tile([P, P], BF16, name="ident_bf")
        make_identity(nc, ident_bf[:])
        warm_in = const.tile([P, 1], F32, name="warm_in")
        warm_out = const.tile([P, 1], F32, name="warm_out")
        nc.vector.memset(warm_in[:], 0.0)
        nc.scalar.activation(out=warm_out[:], in_=warm_in[:], func=ACTF.Exp)

        stat = const.tile([P, P], F32, name="stat")
        nc.vector.memset(stat[:], 0.0)
        x_by_d = xb[:].rearrange("p j d -> p d j")
        nc.vector.tensor_reduce(out=stat[:, 0:D], in_=x_by_d, axis=AX.X, op=ALU.max)
        mn_part = const.tile([P, D], F32, name="mn_part")
        nc.vector.tensor_reduce(out=mn_part[:], in_=x_by_d, axis=AX.X, op=ALU.min)
        nc.vector.tensor_scalar(
            out=stat[:, D : 2 * D], in0=mn_part[:], scalar1=-1.0, scalar2=None, op0=ALU.mult
        )
        stat_t = ps_l.tile([P, P], F32, name="stat_t", tag="L")
        nc.tensor.transpose(stat_t[:], stat[:], ident[:])
        stat_col = const.tile([P, 1], F32, name="stat_col")
        nc.vector.tensor_reduce(out=stat_col[:], in_=stat_t[:], axis=AX.X, op=ALU.max)
        stat_all = ps_l.tile([P, P], F32, name="stat_all", tag="L")
        nc.tensor.transpose(stat_all[:], stat_col[:, 0:1].to_broadcast([P, P]), ident[:])
        mxmn = const.tile([P, 2 * D], F32, name="mxmn")
        nc.vector.tensor_copy(out=mxmn[:], in_=stat_all[:, 0 : 2 * D])
        span = const.tile([P, D], F32, name="span")
        nc.vector.tensor_tensor(
            out=span[:], in0=mxmn[:, 0:D], in1=mxmn[:, D : 2 * D], op=ALU.add
        )
        inv = const.tile([P, D], F32, name="inv")
        nc.vector.reciprocal(inv[:], span[:])
        xs = const.tile([P, NT, D], F32, name="xs")
        nc.vector.tensor_tensor(
            out=xs[:],
            in0=xb[:],
            in1=mxmn[:, D : 2 * D].unsqueeze(1).to_broadcast([P, NT, D]),
            op=ALU.add,
        )
        nc.vector.tensor_tensor(
            out=xs[:], in0=xs[:], in1=inv[:].unsqueeze(1).to_broadcast([P, NT, D]), op=ALU.mult
        )
        nhx = const.tile([P, NT, D], F32, name="nhx")
        nc.vector.tensor_scalar(
            out=nhx[:], in0=xs[:], scalar1=-0.5, scalar2=None, op0=ALU.mult
        )

        zf = const.tile([P, PASSES, PACK, D], F32, name="zf")
        nc.vector.tensor_copy(out=zf[:], in_=zb[:])
        zt = const.tile([P, D, M], BF16, name="zt")
        hz = {}
        cx = {}
        flip = [0]

        def leave_bank(dst, src):
            if flip[0] % 2 == 0:
                nc.scalar.copy(out=dst, in_=src)
            else:
                nc.vector.tensor_copy(out=dst, in_=src)
            flip[0] += 1

        def spread(dst, col_of, dtype, eye):
            for g in range(PASSES):
                bank = ps_o.tile([P, PACK, P], dtype, name="bank", tag="O")
                for t in range(PACK):
                    nc.tensor.transpose(
                        bank[:, t, :], col_of(g, t).to_broadcast([P, P]), eye[:]
                    )
                leave_bank(
                    dst[:, g * HALF : (g + 1) * HALF], bank[:].rearrange("p t n -> p (t n)")
                )

        def spread_dim(d):
            bank = ps_o.tile([P, PASSES * PACK, P], BF16, name="zbank", tag="O")
            for g in range(PASSES):
                for t in range(PACK):
                    nc.tensor.transpose(
                        bank[:, PACK * g + t, :],
                        zb[:, g, t, d : d + 1].to_broadcast([P, P]),
                        ident_bf[:],
                    )
            leave_bank(zt[:, d, :], bank[:].rearrange("p b n -> p (b n)"))

        def spread_half_sums(k):
            hsum = const.tile([P, PASSES, PACK], F32, name="hsum%d" % k)
            nc.vector.tensor_reduce(out=hsum[:], in_=zf[:, :, :, 0:k], axis=AX.X, op=ALU.add)
            hneg = const.tile([P, PASSES, PACK], F32, name="hneg%d" % k)
            nc.vector.tensor_scalar(
                out=hneg[:], in0=hsum[:], scalar1=-0.5, scalar2=None, op0=ALU.mult
            )
            hz[k] = const.tile([P, M], F32, name="hz%d" % k)
            spread(hz[k], lambda g, t: hneg[:, g, t : t + 1], F32, ident)
            cx[k] = const.tile([P, NT], F32, name="cx%d" % k)
            nc.vector.tensor_reduce(out=cx[k][:], in_=nhx[:, :, 0:k], axis=AX.X, op=ALU.add)

        spread_half_sums(5)
        for d in (0, 5, 4, 1, 6, 2, 7, 3):
            spread_dim(d)
        spread_half_sums(6)

        cgrp = const.tile([P, PASSES, COLS, PACK], BF16, name="cgrp", align_bytes=64)
        c_codes = const.tile([P, PASSES, COLS], U32, name="c_codes", align_bytes=64)
        c_scales = const.tile([P, PASSES, COLS], U8, name="c_scales", align_bytes=64)

        def regroup_c(piece):
            g, h = divmod(piece, 2)
            cols = slice(h * HALF, (h + 1) * HALF)
            nc.scalar.copy(
                out=cgrp[:, g, cols, :].rearrange("p (c i) t -> p c t i", i=4),
                in_=craw[:, g, :, cols].rearrange("p t (c i) -> p c t i", i=4),
            )

        def quantise_c(g):
            nc.vector.quantize_mx(
                out=c_codes[:, g, :].bitcast(FP8X4),
                scales=c_scales[:, g, :],
                in_=cgrp[:, g].rearrange("p c t -> p (c t)"),
            )

        out_view = out.rearrange("(p j) c -> j p c", j=NT)
        terms = {}
        banks = {}
        groups = {}
        quant = {}
        sums = {}

        def stage_terms(j):
            k = D - n_abs_of(j)
            n_chain = n_chain_of(j)
            n_leaf = k - n_chain
            abs_leaves = []
            for d in range(k, D):
                leaf = terms_pool.tile([P, M], F32, name="abs%d" % (d - k))
                nc.scalar.activation(
                    out=leaf[:],
                    in_=zt[:, d, :],
                    func=ACTF.Abs,
                    bias=nhx[:, j, d : d + 1],
                    scale=0.5,
                )
                abs_leaves.append(leaf)
            acc = terms_pool.tile([P, M], F32, name="acc")
            max_leaves = []
            for d in range(max(n_chain, n_leaf)):
                if d == 3 and 0 <= j - 3:
                    stage_quant(j - 3)
                if d < n_chain:
                    nc.vector.scalar_tensor_tensor(
                        out=acc[:],
                        in0=zt[:, d, :],
                        scalar=xs[:, j, d : d + 1],
                        in1=(hz[k][:] if d == 0 else acc[:]),
                        op0=ALU.max,
                        op1=ALU.add,
                    )
                if d < n_leaf:
                    e = n_chain + d
                    max_leaf = terms_pool.tile([P, M], F32, name="max_leaf%d" % d)
                    if d == 0:
                        nc.vector.tensor_scalar(
                            out=max_leaf[:],
                            in0=zt[:, e, :],
                            scalar1=xs[:, j, e : e + 1],
                            scalar2=cx[k][:, j : j + 1],
                            op0=ALU.max,
                            op1=ALU.add,
                        )
                    else:
                        nc.vector.tensor_scalar(
                            out=max_leaf[:],
                            in0=zt[:, e, :],
                            scalar1=xs[:, j, e : e + 1],
                            scalar2=None,
                            op0=ALU.max,
                        )
                    max_leaves.append(max_leaf)
            terms[j] = abs_leaves[:1] + max_leaves[:1] + abs_leaves[1:] + max_leaves[1:2] + [acc] + max_leaves[2:]

        def stage_sum(j):
            made = terms[j]
            last = len(made) - 1
            pair = []
            for g in range(PASSES):
                bank = ps_l.tile([P, PACK, P], F32, name="l1t", tag="L")
                pair.append(bank)
            for i, term in enumerate(made):
                for g in range(PASSES):
                    for t in range(PACK):
                        b = PACK * g + t
                        nc.tensor.matmul(
                            pair[g][:, t, :],
                            lhsT=term[:, b * P : (b + 1) * P],
                            rhs=ident[:],
                            is_transpose=True,
                            start=(i == 0 and t == 0),
                            stop=(i == last and t == PACK - 1),
                        )
            banks[j] = pair

        def stage_exp(j):
            grp = work.tile([P, PASSES, P, PACK], BF16, name="grp", align_bytes=64)
            for g, bank in enumerate(banks[j]):
                nc.scalar.activation(
                    out=grp[:, g],
                    in_=bank[:].rearrange("p t n -> p n t"),
                    func=ACTF.Exp,
                    scale=-2.0,
                )
            groups[j] = grp

        def stage_quant(j):
            grp = groups[j]
            codes = work.tile([P, PASSES * P], U32, name="codes", align_bytes=64, bufs=4)
            scales = work.tile([P, PASSES * P], U8, name="scales", align_bytes=64, bufs=4)
            nc.vector.quantize_mx(
                out=codes[:].bitcast(FP8X4),
                scales=scales[:],
                in_=grp[:].rearrange("p g n t -> p (g n t)"),
            )
            quant[j] = (codes, scales)

        def stage_mx(j):
            codes, scales = quant[j]
            sums[j] = []
            for h in range(COLS // HALF):
                acc = ps_o.tile([P, HALF], F32, name="osum", tag="O")
                for g in range(PASSES):
                    nc.tensor.matmul_mx(
                        out=acc[:],
                        lhsT=codes[:, g * P : (g + 1) * P].bitcast(FP8X4),
                        lhsT_scale=scales[:, g * P : (g + 1) * P],
                        rhs=c_codes[:, g, h * HALF : (h + 1) * HALF].bitcast(FP8X4),
                        rhs_scale=c_scales[:, g, h * HALF : (h + 1) * HALF],
                        start=(g == 0),
                        stop=(g == PASSES - 1),
                    )
                sums[j].append(acc)

        def stage_store(j):
            res = work.tile([P, COLS], F32, name="res")
            for h, acc in enumerate(sums[j]):
                cols = slice(h * HALF, (h + 1) * HALF)
                if j >= NT - 2 and h == 1:
                    nc.vector.tensor_copy(out=res[:, cols], in_=acc[:])
                else:
                    nc.scalar.copy(out=res[:, cols], in_=acc[:])
                if j == NT - 1:
                    nc.sync.dma_start(out=out_view[j][:, cols], in_=res[:, cols])
            if j < NT - 1:
                nc.sync.dma_start(out=out_view[j], in_=res[:])

        with tc.manual_schedule():
            for i in range(NT + 5):
                if 0 <= i - 3 < NT and not (i < NT and n_chain_of(i) == 4):
                    stage_quant(i - 3)
                if 0 <= i - 2 < NT:
                    stage_exp(i - 2)
                if 0 <= i - 5 < NT:
                    stage_store(i - 5)
                if i < NT:
                    stage_terms(i)
                if i == 0:
                    regroup_c(0)
                if i < 3:
                    regroup_c(i + 1)
                if i == 3:
                    quantise_c(0)
                    quantise_c(1)
                if 0 <= i - 1 < NT:
                    stage_sum(i - 1)
                if i % 2 == 0 and 0 <= i - 4 < NT:
                    stage_mx(i - 4)
                    stage_mx(i - 3)
